import numpy as np
import ml_dtypes


def mxq(x, axis, fmt="e4m3"):
    dtype, down = {"e4m3": (ml_dtypes.float8_e4m3fn, 7), "e5m2": (ml_dtypes.float8_e5m2, 14)}[fmt]
    v = np.moveaxis(np.asarray(x, np.float32).astype(ml_dtypes.bfloat16).astype(np.float64), axis, -1)
    blocks = v.reshape(v.shape[:-1] + (-1, 32))
    amax = np.abs(blocks).max(-1, keepdims=True)
    byte = np.maximum(np.where(amax > 0, np.frexp(amax)[1] - 1 + 127, 0) - down, 1)
    scale = np.exp2(byte - 127.0)
    codes = (blocks / scale).astype(np.float32).astype(dtype).astype(np.float64)
    return np.moveaxis((codes * scale).reshape(v.shape), -1, axis)


WIDE = False


def mx_kscale(k):
    if not WIDE:
        return np.ones(k)
    levels = np.array([10, -10, 5, -5, 0])
    a = np.random.permutation(np.resize(levels, k // 512 * 4)).reshape(k // 512, 4)
    idx = np.arange(k)
    return np.exp2(a[idx // 512, idx % 128 // 32])


BF16 = ml_dtypes.bfloat16


def bf(x):
    return np.asarray(x, np.float32).astype(BF16)


def f64(x):
    return np.asarray(x).astype(np.float64)


B, S, C, H, P = 2, 512, 512, 128, 512
G2, G3 = 2, 4


def softmax(z, axis):
    e = np.exp(z - z.max(axis=axis, keepdims=True))
    return e / e.sum(axis=axis, keepdims=True)


def channel_map(q, k):
    return softmax(f64(q) @ f64(k).transpose(0, 2, 1) / np.sqrt(H), -1)


def setup_inputs():
    t = mx_kscale(S)
    return {"q1": bf(np.random.standard_normal((B, C, H)) * 2.0), "k1": bf(np.random.standard_normal((B, C, H)) * 2.0),
            "q2": bf(np.random.standard_normal((G2 * B, C, H)) * 2.0), "k2": bf(np.random.standard_normal((G2 * B, C, H)) * 2.0),
            "q3": bf(np.random.standard_normal((G3 * B, C, H)) * 2.0), "k3": bf(np.random.standard_normal((G3 * B, C, H)) * 2.0),
            "v": bf(np.random.standard_normal((B, C, S)) * t),
            "wo": bf(np.random.standard_normal((S, P)) * 2.0 / np.sqrt(S) / t[:, None]),
            "bo": bf(np.random.standard_normal(P) * 0.2)}


def reference(q1, k1, q2, k2, q3, k3, v, wo, bo):
    a1 = channel_map(q1, k1)
    a2 = channel_map(q2, k2).reshape(B, G2, C, C).mean(axis=1)
    a3 = channel_map(q3, k3).reshape(B, G3, C, C).mean(axis=1)
    stacked = np.stack([a1, a2, a3], axis=0)
    gate = softmax(stacked, 0)
    attn = (stacked * gate).sum(axis=0)
    h = mxq(attn, 2, "e4m3") @ mxq(f64(v), 1, "e4m3")
    out = (mxq(h, 2, "e4m3") @ mxq(f64(wo), 0, "e4m3")) + f64(bo)
    return out.transpose(0, 2, 1)

@@ -1,0 +1,286 @@
+from contextlib import ExitStack
+import math
+
+import concourse.mybir as mybir
+from concourse.masks import make_identity
+
+F32 = mybir.dt.float32
+BF16 = mybir.dt.bfloat16
+U32 = mybir.dt.uint32
+U8 = mybir.dt.uint8
+FP8X4 = mybir.dt.float8_e4m3fn_x4
+ACT = mybir.ActivationFunctionType
+ALU = mybir.AluOpType
+AXIS = mybir.AxisListType
+
+P = 128
+PACK = 4
+B, C, H, S, PO = 2, 512, 128, 512, 512
+BLOCKS = C // P
+UNITS = B * BLOCKS
+GROUP_SIZES = (1, 2, 4)
+SCALES = len(GROUP_SIZES)
+MAPS = sum(GROUP_SIZES)
+FIRST_MAP = tuple(sum(GROUP_SIZES[:i]) for i in range(SCALES))
+LAST_MAP = tuple(FIRST_MAP[i] + GROUP_SIZES[i] - 1 for i in range(SCALES))
+GROUP_OF = tuple(i for i in range(SCALES) for m in range(GROUP_SIZES[i]))
+SCORE_SCALE = 1.0 / math.sqrt(H)
+TOTAL = UNITS * MAPS
+
+AHEAD = 2
+LAG = MAPS + 5
+PROJECT_LAG = 2
+
+FLOPS = 2 * B * MAPS * C * C * H + 2 * B * C * C * S + 2 * B * C * S * PO
+
+
+def tile_channeldeattention_pa_kernel(tc, q1, k1, q2, k2, q3, k3, v, wo, bo, out):
+    nc = tc.nc
+    queries = (q1, q2, q3)
+    keys = (k1, k2, k3)
+
+    with ExitStack() as ctx:
+        consts = ctx.enter_context(tc.tile_pool(name="consts", bufs=1))
+        raw = ctx.enter_context(tc.tile_pool(name="raw", bufs=MAPS))
+        operands = ctx.enter_context(tc.tile_pool(name="operands", bufs=MAPS))
+        weights = ctx.enter_context(tc.tile_pool(name="weights", bufs=1))
+        stream = ctx.enter_context(tc.tile_pool(name="stream", bufs=10))
+        kept = ctx.enter_context(tc.tile_pool(name="kept", bufs=UNITS))
+        sample = ctx.enter_context(tc.tile_pool(name="sample", bufs=B))
+        results = ctx.enter_context(tc.tile_pool(name="results", bufs=4))
+        psum = ctx.enter_context(tc.psum_pool(name="psum", bufs=8))
+        ctx.enter_context(tc.manual_schedule())
+
+        ident_bf = consts.tile([P, P], BF16)
+        make_identity(nc, ident_bf[:])
+        ident_f = consts.tile([P, P], F32)
+        make_identity(nc, ident_f[:])
+        mean_weight = consts.tile([P, MAPS], F32)
+        for i in range(SCALES):
+            nc.vector.memset(mean_weight[:, FIRST_MAP[i] : LAST_MAP[i] + 1], 1.0 / GROUP_SIZES[i])
+        bo_rows = consts.tile([P, P], BF16)
+        nc.vector.memset(bo_rows[:], 0.0)
+
+        raw_tiles = {}
+        transposed = {}
+        sums = {}
+        mean_inverse = {}
+        ratio = {}
+        inverse = {}
+        folded = {}
+        gate_exp = {}
+        spare = {}
+
+        def load_map(b, j):
+            i = GROUP_OF[j]
+            n = b * GROUP_SIZES[i] + j - FIRST_MAP[i]
+            q_raw = raw.tile([P, BLOCKS, H], BF16)
+            nc.sync.dma_start(out=q_raw[:], in_=queries[i][n : n + 1].rearrange("o (a p) h -> p (o a) h", p=P))
+            k_raw = raw.tile([P, PACK, H], BF16)
+            nc.sync.dma_start(out=k_raw[:], in_=keys[i][n : n + 1].rearrange("o (p t) h -> (o p) t h", t=PACK))
+            raw_tiles[(b, j)] = (q_raw, k_raw)
+
+        def transpose_map(b, j):
+            q_raw, k_raw = raw_tiles[(b, j)]
+            q_bank = psum.tile([P, BLOCKS, P], BF16, tag="bank")
+            for a in range(BLOCKS):
+                nc.tensor.transpose(q_bank[:, a, :], q_raw[:, a, :], ident_bf[:])
+            k_bank = psum.tile([P, PACK, P], BF16, tag="bank")
+            for t in range(PACK):
+                nc.tensor.transpose(k_bank[:, t, :], k_raw[:, t, :], ident_bf[:])
+            q_t = operands.tile([P, BLOCKS, P], BF16)
+            nc.vector.tensor_copy(out=q_t[:], in_=q_bank[:])
+            k_t = operands.tile([P, PACK, P], BF16)
+            nc.scalar.copy(out=k_t[:], in_=k_bank[:])
+            transposed[(b, j)] = (q_t, k_t)
+
+        def score_tile(u, j):
+            b, a = divmod(u, BLOCKS)
+            i = GROUP_OF[j]
+            if j == 0:
+                sums[u] = kept.tile([P, MAPS], F32, name="sums")
+                folded[u] = kept.tile([P, SCALES, C], F32, name="folded")
+            q_t, k_t = transposed[(b, j)]
+            scores = psum.tile([P, C], F32, tag="bank")
+            nc.tensor.matmul(
+                out=scores[:], lhsT=q_t[:, a, :], rhs=k_t[:].rearrange("h t c -> h (t c)"), start=True, stop=True
+            )
+            row_max = stream.tile([P, 1], F32)
+            nc.vector.tensor_reduce(out=row_max[:], in_=scores[:], axis=AXIS.X, op=ALU.max)
+            shift = stream.tile([P, 1], F32)
+            nc.gpsimd.tensor_scalar(
+                out=shift[:], in0=row_max[:], scalar1=-SCORE_SCALE, scalar2=0.0, op0=ALU.mult, op1=ALU.add
+            )
+            if j == FIRST_MAP[i]:
+                target = folded[u][:, i, :]
+            else:
+                spare[(u, j)] = stream.tile([P, C], F32, name="spare")
+                target = spare[(u, j)][:]
+            nc.scalar.activation(
+                out=target, in_=scores[:], func=ACT.Exp, bias=shift[:], scale=SCORE_SCALE,
+                accum_out=sums[u][:, j : j + 1],
+            )
+
+        def fold_tile(u, j):
+            i = GROUP_OF[j]
+            if j == 0:
+                inverse[u] = kept.tile([P, MAPS], F32, name="inverse")
+                nc.vector.reciprocal(out=inverse[u][:], in_=sums[u][:])
+            if j == 1:
+                mean_inverse[u] = kept.tile([P, MAPS], F32, name="mean_inverse")
+                nc.vector.tensor_tensor(out=mean_inverse[u][:], in0=inverse[u][:], in1=mean_weight[:], op=ALU.mult)
+                ratio[u] = kept.tile([P, MAPS], F32, name="ratio")
+                for g in range(1, SCALES):
+                    nc.vector.tensor_scalar(
+                        out=ratio[u][:, FIRST_MAP[g] + 1 : LAST_MAP[g] + 1],
+                        in0=inverse[u][:, FIRST_MAP[g] + 1 : LAST_MAP[g] + 1],
+                        scalar1=sums[u][:, FIRST_MAP[g] : FIRST_MAP[g] + 1],
+                        scalar2=None,
+                        op0=ALU.mult,
+                    )
+                gate_exp[u] = kept.tile([P, SCALES, C], F32, name="gate_exp")
+            if j > FIRST_MAP[i]:
+                nc.vector.scalar_tensor_tensor(
+                    out=folded[u][:, i, :], in0=spare[(u, j)][:], scalar=ratio[u][:, j : j + 1],
+                    in1=folded[u][:, i, :], op0=ALU.mult, op1=ALU.add,
+                )
+            for g in range(SCALES):
+                if j == max(LAST_MAP[g], 1):
+                    nc.scalar.activation(
+                        out=gate_exp[u][:, g, :], in_=folded[u][:, g, :], func=ACT.Exp,
+                        scale=mean_inverse[u][:, FIRST_MAP[g] : FIRST_MAP[g] + 1],
+                    )
+
+        def flip_and_add(three_maps):
+            bank = psum.tile([P, PACK, P], F32, tag="bank", name="flipped")
+            for t in range(PACK):
+                for g in range(SCALES):
+                    nc.tensor.matmul(
+                        out=bank[:, t, :], lhsT=three_maps[:, g, t * P : (t + 1) * P], rhs=ident_f[:],
+                        is_transpose=True, start=(g == 0), stop=(g == SCALES - 1),
+                    )
+            return bank
+
+        for j in range(MAPS):
+            load_map(0, j)
+        v_raw = weights.tile([P, B, PACK, S], BF16)
+        for b in range(B):
+            nc.sync.dma_start(out=v_raw[:, b], in_=v[b : b + 1].rearrange("o (p j) s -> (o p) j s", j=PACK))
+        wo_raw = weights.tile([P, PACK, PO], BF16)
+        nc.sync.dma_start(out=wo_raw[:], in_=wo.rearrange("(t p) n -> p t n", p=P))
+        nc.sync.dma_start(out=bo_rows[0 : PO // P, :], in_=bo.rearrange("(r m) -> r m", m=P))
+
+        for step in range(-AHEAD, TOTAL + LAG):
+            if 0 <= step < TOTAL:
+                score_tile(step // MAPS, step % MAPS)
+            early = step + AHEAD
+            if early < TOTAL and (early // MAPS) % BLOCKS == 0:
+                b, j = early // (MAPS * BLOCKS), early % MAPS
+                transpose_map(b, j)
+                if b + 1 < B:
+                    load_map(b + 1, j)
+            late = step - LAG
+            if late >= 0:
+                fold_tile(late // MAPS, late % MAPS)
+
+        v_codes = weights.tile([P, B, S], U32, align_bytes=64)
+        v_scales = weights.tile([P, B, S], U8, align_bytes=64)
+        wo_codes = weights.tile([P, PO], U32, align_bytes=64)
+        wo_scales = weights.tile([P, PO], U8, align_bytes=64)
+        grouped = []
+        for rows in (v_raw[:, 0], v_raw[:, 1], wo_raw[:]):
+            side_by_side = weights.tile([P, S, PACK], BF16, align_bytes=64, name="side_by_side", bufs=3)
+            nc.vector.tensor_copy(out=side_by_side[:], in_=rows.rearrange("p j s -> p s j"))
+            grouped.append(side_by_side)
+        for b in range(B):
+            nc.vector.quantize_mx(
+                out=v_codes[:, b, :].bitcast(FP8X4), scales=v_scales[:, b, :],
+                in_=grouped[b][:].rearrange("p s j -> p (s j)"),
+            )
+        nc.vector.quantize_mx(
+            out=wo_codes[:].bitcast(FP8X4), scales=wo_scales[:], in_=grouped[B][:].rearrange("p s j -> p (s j)")
+        )
+        bo_bank = psum.tile([P, P], BF16, tag="bank")
+        nc.tensor.transpose(bo_bank[:], bo_rows[:], ident_bf[:])
+        bias = consts.tile([P, PO // P], F32)
+        nc.vector.tensor_copy(out=bias[:], in_=bo_bank[:, 0 : PO // P])
+
+        gate_inverse = {}
+        for u in range(UNITS):
+            denominator = flip_and_add(gate_exp[u])
+            gate_inverse[u] = kept.tile([P, P, PACK], F32, name="gate_inverse")
+            nc.scalar.activation(out=gate_inverse[u][:], in_=denominator[:].rearrange("p t c -> p c t"), func=ACT.Ln)
+        for u in range(UNITS):
+            nc.scalar.activation(out=gate_inverse[u][:], in_=gate_inverse[u][:], func=ACT.Exp, scale=-1.0)
+        numerator = {}
+        for u in range(UNITS):
+            for g in range(SCALES):
+                nc.vector.scalar_tensor_tensor(
+                    out=folded[u][:, g, :], in0=folded[u][:, g, :],
+                    scalar=mean_inverse[u][:, FIRST_MAP[g] : FIRST_MAP[g] + 1],
+                    in1=gate_exp[u][:, g, :], op0=ALU.mult, op1=ALU.mult,
+                )
+            numerator[u] = flip_and_add(folded[u])
+
+        attn = {}
+        attn_codes = {}
+        attn_scales = {}
+        hidden = {}
+        for step in range(UNITS + 1 + PROJECT_LAG):
+            if step < UNITS:
+                b, a = divmod(step, BLOCKS)
+                if a == 0:
+                    attn[b] = sample.tile([P, C, PACK], BF16, align_bytes=64, name="attn")
+                    attn_codes[b] = sample.tile([P, C], U32, align_bytes=64, name="attn_codes")
+                    attn_scales[b] = sample.tile([P, C], U8, align_bytes=64, name="attn_scales")
+                    hidden[b] = sample.tile([P, C, PACK], BF16, align_bytes=64, name="hidden")
+                nc.vector.tensor_tensor(
+                    out=attn[b][:, a * P : (a + 1) * P, :], in0=numerator[step][:].rearrange("p t c -> p c t"),
+                    in1=gate_inverse[step][:], op=ALU.mult,
+                )
+            if 0 <= step - 1 < UNITS:
+                b, a = divmod(step - 1, BLOCKS)
+                cols = slice(a * P, (a + 1) * P)
+                nc.vector.quantize_mx(
+                    out=attn_codes[b][:, cols].bitcast(FP8X4), scales=attn_scales[b][:, cols],
+                    in_=attn[b][:, cols, :].rearrange("p c t -> p (c t)"),
+                )
+                h_bank = psum.tile([P, PACK, P], F32, tag="bank")
+                for t in range(PACK):
+                    nc.tensor.matmul_mx(
+                        out=h_bank[:, t, :],
+                        lhsT=v_codes[:, b, t * P : (t + 1) * P].bitcast(FP8X4),
+                        lhsT_scale=v_scales[:, b, t * P : (t + 1) * P],
+                        rhs=attn_codes[b][:, cols].bitcast(FP8X4),
+                        rhs_scale=attn_scales[b][:, cols],
+                        start=True, stop=True,
+                    )
+                nc.scalar.copy(out=hidden[b][:, cols, :], in_=h_bank[:].rearrange("p t c -> p c t"))
+            done = step - 1 - PROJECT_LAG
+            if done >= 0 and done % BLOCKS == BLOCKS - 1:
+                b = done // BLOCKS
+                h_codes = sample.tile([P, C], U32, align_bytes=64)
+                h_scales = sample.tile([P, C], U8, align_bytes=64)
+                nc.vector.quantize_mx(
+                    out=h_codes[:].bitcast(FP8X4), scales=h_scales[:], in_=hidden[b][:].rearrange("p c t -> p (c t)")
+                )
+                for r in range(PO // P):
+                    o_bank = psum.tile([P, C], F32, tag="bank")
+                    nc.tensor.matmul_mx(
+                        out=o_bank[:],
+                        lhsT=wo_codes[:, r * P : (r + 1) * P].bitcast(FP8X4),
+                        lhsT_scale=wo_scales[:, r * P : (r + 1) * P],
+                        rhs=h_codes[:].bitcast(FP8X4),
+                        rhs_scale=h_scales[:],
+                        start=True, stop=True,
+                    )
+                    result = results.tile([P, C], F32)
+                    if r % 2 == 0:
+                        nc.scalar.activation(out=result[:], in_=o_bank[:], func=ACT.Identity, bias=bias[:, r : r + 1])
+                    else:
+                        nc.vector.tensor_scalar(
+                            out=result[:], in0=o_bank[:], scalar1=bias[:, r : r + 1], scalar2=None, op0=ALU.add
+                        )
+                    nc.sync.dma_start(
+                        out=out[b : b + 1, r * P : (r + 1) * P, :].rearrange("o m c -> (o m) c"), in_=result[:]
+                    )

@@ -82,17 +82,14 @@ def tile_channeldeattention_pa_kernel(tc, q1, k1, q2, k2, q3, k3, v, wo, bo, out
 
         def transpose_map(b, j):
             q_raw, k_raw = raw_tiles[(b, j)]
-            q_bank = psum.tile([P, BLOCKS, P], BF16, tag="bank")
+            qk_bank = psum.tile([P, 2, BLOCKS, P], BF16, tag="bank")
             for a in range(BLOCKS):
-                nc.tensor.transpose(q_bank[:, a, :], q_raw[:, a, :], ident_bf[:])
-            k_bank = psum.tile([P, PACK, P], BF16, tag="bank")
+                nc.tensor.transpose(qk_bank[:, 0, a, :], q_raw[:, a, :], ident_bf[:])
             for t in range(PACK):
-                nc.tensor.transpose(k_bank[:, t, :], k_raw[:, t, :], ident_bf[:])
-            q_t = operands.tile([P, BLOCKS, P], BF16)
-            nc.vector.tensor_copy(out=q_t[:], in_=q_bank[:])
-            k_t = operands.tile([P, PACK, P], BF16)
-            nc.scalar.copy(out=k_t[:], in_=k_bank[:])
-            transposed[(b, j)] = (q_t, k_t)
+                nc.tensor.transpose(qk_bank[:, 1, t, :], k_raw[:, t, :], ident_bf[:])
+            qk_t = operands.tile([P, 2, BLOCKS, P], BF16)
+            nc.scalar.copy(out=qk_t[:], in_=qk_bank[:])
+            transposed[(b, j)] = (qk_t[:, 0], qk_t[:, 1])
 
         def score_tile(u, j):
             b, a = divmod(u, BLOCKS)
@@ -103,7 +100,7 @@ def tile_channeldeattention_pa_kernel(tc, q1, k1, q2, k2, q3, k3, v, wo, bo, out
             q_t, k_t = transposed[(b, j)]
             scores = psum.tile([P, C], F32, tag="bank")
             nc.tensor.matmul(
-                out=scores[:], lhsT=q_t[:, a, :], rhs=k_t[:].rearrange("h t c -> h (t c)"), start=True, stop=True
+                out=scores[:], lhsT=q_t[:, a, :], rhs=k_t.rearrange("h t c -> h (t c)"), start=True, stop=True
             )
             row_max = stream.tile([P, 1], F32)
             nc.vector.tensor_reduce(out=row_max[:], in_=scores[:], axis=AXIS.X, op=ALU.max)
@@ -126,17 +123,17 @@ def tile_channeldeattention_pa_kernel(tc, q1, k1, q2, k2, q3, k3, v, wo, bo, out
             if j == 0:
                 inverse[u] = kept.tile([P, MAPS], F32, name="inverse")
                 nc.vector.reciprocal(out=inverse[u][:], in_=sums[u][:])
-            if j == 1:
                 mean_inverse[u] = kept.tile([P, MAPS], F32, name="mean_inverse")
-                nc.vector.tensor_tensor(out=mean_inverse[u][:], in0=inverse[u][:], in1=mean_weight[:], op=ALU.mult)
+                nc.gpsimd.tensor_tensor(out=mean_inverse[u][:], in0=inverse[u][:], in1=mean_weight[:], op=ALU.mult)
                 ratio[u] = kept.tile([P, MAPS], F32, name="ratio")
                 for g in range(1, SCALES):
-                    nc.vector.tensor_scalar(
+                    nc.gpsimd.tensor_scalar(
                         out=ratio[u][:, FIRST_MAP[g] + 1 : LAST_MAP[g] + 1],
                         in0=inverse[u][:, FIRST_MAP[g] + 1 : LAST_MAP[g] + 1],
                         scalar1=sums[u][:, FIRST_MAP[g] : FIRST_MAP[g] + 1],
-                        scalar2=None,
+                        scalar2=0.0,
                         op0=ALU.mult,
+                        op1=ALU.add,
                     )
                 gate_exp[u] = kept.tile([P, SCALES, C], F32, name="gate_exp")
             if j > FIRST_MAP[i]:

@@ -82,14 +82,17 @@ def tile_channeldeattention_pa_kernel(tc, q1, k1, q2, k2, q3, k3, v, wo, bo, out
 
         def transpose_map(b, j):
             q_raw, k_raw = raw_tiles[(b, j)]
-            qk_bank = psum.tile([P, 2, BLOCKS, P], BF16, tag="bank")
+            q_bank = psum.tile([P, BLOCKS, P], BF16, tag="bank")
             for a in range(BLOCKS):
-                nc.tensor.transpose(qk_bank[:, 0, a, :], q_raw[:, a, :], ident_bf[:])
+                nc.tensor.transpose(q_bank[:, a, :], q_raw[:, a, :], ident_bf[:])
+            k_bank = psum.tile([P, PACK, P], BF16, tag="bank")
             for t in range(PACK):
-                nc.tensor.transpose(qk_bank[:, 1, t, :], k_raw[:, t, :], ident_bf[:])
-            qk_t = operands.tile([P, 2, BLOCKS, P], BF16)
-            nc.scalar.copy(out=qk_t[:], in_=qk_bank[:])
-            transposed[(b, j)] = (qk_t[:, 0], qk_t[:, 1])
+                nc.tensor.transpose(k_bank[:, t, :], k_raw[:, t, :], ident_bf[:])
+            q_t = operands.tile([P, BLOCKS, P], BF16)
+            nc.vector.tensor_copy(out=q_t[:], in_=q_bank[:])
+            k_t = operands.tile([P, PACK, P], BF16)
+            nc.scalar.copy(out=k_t[:], in_=k_bank[:])
+            transposed[(b, j)] = (q_t, k_t)
 
         def score_tile(u, j):
             b, a = divmod(u, BLOCKS)
@@ -100,7 +103,7 @@ def tile_channeldeattention_pa_kernel(tc, q1, k1, q2, k2, q3, k3, v, wo, bo, out
             q_t, k_t = transposed[(b, j)]
             scores = psum.tile([P, C], F32, tag="bank")
             nc.tensor.matmul(
-                out=scores[:], lhsT=q_t[:, a, :], rhs=k_t.rearrange("h t c -> h (t c)"), start=True, stop=True
+                out=scores[:], lhsT=q_t[:, a, :], rhs=k_t[:].rearrange("h t c -> h (t c)"), start=True, stop=True
             )
             row_max = stream.tile([P, 1], F32)
             nc.vector.tensor_reduce(out=row_max[:], in_=scores[:], axis=AXIS.X, op=ALU.max)
@@ -123,17 +126,17 @@ def tile_channeldeattention_pa_kernel(tc, q1, k1, q2, k2, q3, k3, v, wo, bo, out
             if j == 0:
                 inverse[u] = kept.tile([P, MAPS], F32, name="inverse")
                 nc.vector.reciprocal(out=inverse[u][:], in_=sums[u][:])
+            if j == 1:
                 mean_inverse[u] = kept.tile([P, MAPS], F32, name="mean_inverse")
-                nc.gpsimd.tensor_tensor(out=mean_inverse[u][:], in0=inverse[u][:], in1=mean_weight[:], op=ALU.mult)
+                nc.vector.tensor_tensor(out=mean_inverse[u][:], in0=inverse[u][:], in1=mean_weight[:], op=ALU.mult)
                 ratio[u] = kept.tile([P, MAPS], F32, name="ratio")
                 for g in range(1, SCALES):
-                    nc.gpsimd.tensor_scalar(
+                    nc.vector.tensor_scalar(
                         out=ratio[u][:, FIRST_MAP[g] + 1 : LAST_MAP[g] + 1],
                         in0=inverse[u][:, FIRST_MAP[g] + 1 : LAST_MAP[g] + 1],
                         scalar1=sums[u][:, FIRST_MAP[g] : FIRST_MAP[g] + 1],
-                        scalar2=0.0,
+                        scalar2=None,
                         op0=ALU.mult,
-                        op1=ALU.add,
                     )
                 gate_exp[u] = kept.tile([P, SCALES, C], F32, name="gate_exp")
             if j > FIRST_MAP[i]:
@@ -187,16 +190,8 @@ def tile_channeldeattention_pa_kernel(tc, q1, k1, q2, k2, q3, k3, v, wo, bo, out
         grouped = []
         for rows in (v_raw[:, 0], v_raw[:, 1], wo_raw[:]):
             side_by_side = weights.tile([P, S, PACK], BF16, align_bytes=64, name="side_by_side", bufs=3)
-            nc.vector.tensor_copy(out=side_by_side[:], in_=rows.rearrange("p j s -> p s j"))
+            nc.scalar.copy(out=side_by_side[:], in_=rows.rearrange("p j s -> p s j"))
             grouped.append(side_by_side)
-        for b in range(B):
-            nc.vector.quantize_mx(
-                out=v_codes[:, b, :].bitcast(FP8X4), scales=v_scales[:, b, :],
-                in_=grouped[b][:].rearrange("p s j -> p (s j)"),
-            )
-        nc.vector.quantize_mx(
-            out=wo_codes[:].bitcast(FP8X4), scales=wo_scales[:], in_=grouped[B][:].rearrange("p s j -> p (s j)")
-        )
         bo_bank = psum.tile([P, P], BF16, tag="bank")
         nc.tensor.transpose(bo_bank[:], bo_rows[:], ident_bf[:])
         bias = consts.tile([P, PO // P], F32)
@@ -218,6 +213,14 @@ def tile_channeldeattention_pa_kernel(tc, q1, k1, q2, k2, q3, k3, v, wo, bo, out
                     in1=gate_exp[u][:, g, :], op0=ALU.mult, op1=ALU.mult,
                 )
             numerator[u] = flip_and_add(folded[u])
+        for b in range(B):
+            nc.vector.quantize_mx(
+                out=v_codes[:, b, :].bitcast(FP8X4), scales=v_scales[:, b, :],
+                in_=grouped[b][:].rearrange("p s j -> p (s j)"),
+            )
+        nc.vector.quantize_mx(
+            out=wo_codes[:].bitcast(FP8X4), scales=wo_scales[:], in_=grouped[B][:].rearrange("p s j -> p (s j)")
+        )
 
         attn = {}
         attn_codes = {}

@@ -82,17 +82,14 @@ def tile_channeldeattention_pa_kernel(tc, q1, k1, q2, k2, q3, k3, v, wo, bo, out
 
         def transpose_map(b, j):
             q_raw, k_raw = raw_tiles[(b, j)]
-            q_bank = psum.tile([P, BLOCKS, P], BF16, tag="bank")
+            qk_bank = psum.tile([P, 2, BLOCKS, P], BF16, tag="bank")
             for a in range(BLOCKS):
-                nc.tensor.transpose(q_bank[:, a, :], q_raw[:, a, :], ident_bf[:])
-            k_bank = psum.tile([P, PACK, P], BF16, tag="bank")
+                nc.tensor.transpose(qk_bank[:, 0, a, :], q_raw[:, a, :], ident_bf[:])
             for t in range(PACK):
-                nc.tensor.transpose(k_bank[:, t, :], k_raw[:, t, :], ident_bf[:])
-            q_t = operands.tile([P, BLOCKS, P], BF16)
-            nc.vector.tensor_copy(out=q_t[:], in_=q_bank[:])
-            k_t = operands.tile([P, PACK, P], BF16)
-            nc.scalar.copy(out=k_t[:], in_=k_bank[:])
-            transposed[(b, j)] = (q_t, k_t)
+                nc.tensor.transpose(qk_bank[:, 1, t, :], k_raw[:, t, :], ident_bf[:])
+            qk_t = operands.tile([P, 2, BLOCKS, P], BF16)
+            nc.vector.tensor_copy(out=qk_t[:], in_=qk_bank[:])
+            transposed[(b, j)] = (qk_t[:, 0], qk_t[:, 1])
 
         def score_tile(u, j):
             b, a = divmod(u, BLOCKS)
@@ -103,7 +100,7 @@ def tile_channeldeattention_pa_kernel(tc, q1, k1, q2, k2, q3, k3, v, wo, bo, out
             q_t, k_t = transposed[(b, j)]
             scores = psum.tile([P, C], F32, tag="bank")
             nc.tensor.matmul(
-                out=scores[:], lhsT=q_t[:, a, :], rhs=k_t[:].rearrange("h t c -> h (t c)"), start=True, stop=True
+                out=scores[:], lhsT=q_t[:, a, :], rhs=k_t.rearrange("h t c -> h (t c)"), start=True, stop=True
             )
             row_max = stream.tile([P, 1], F32)
             nc.vector.tensor_reduce(out=row_max[:], in_=scores[:], axis=AXIS.X, op=ALU.max)
@@ -190,8 +187,16 @@ def tile_channeldeattention_pa_kernel(tc, q1, k1, q2, k2, q3, k3, v, wo, bo, out
         grouped = []
         for rows in (v_raw[:, 0], v_raw[:, 1], wo_raw[:]):
             side_by_side = weights.tile([P, S, PACK], BF16, align_bytes=64, name="side_by_side", bufs=3)
-            nc.scalar.copy(out=side_by_side[:], in_=rows.rearrange("p j s -> p s j"))
+            nc.vector.tensor_copy(out=side_by_side[:], in_=rows.rearrange("p j s -> p s j"))
             grouped.append(side_by_side)
+        for b in range(B):
+            nc.vector.quantize_mx(
+                out=v_codes[:, b, :].bitcast(FP8X4), scales=v_scales[:, b, :],
+                in_=grouped[b][:].rearrange("p s j -> p (s j)"),
+            )
+        nc.vector.quantize_mx(
+            out=wo_codes[:].bitcast(FP8X4), scales=wo_scales[:], in_=grouped[B][:].rearrange("p s j -> p (s j)")
+        )
         bo_bank = psum.tile([P, P], BF16, tag="bank")
         nc.tensor.transpose(bo_bank[:], bo_rows[:], ident_bf[:])
         bias = consts.tile([P, PO // P], F32)
@@ -213,14 +218,6 @@ def tile_channeldeattention_pa_kernel(tc, q1, k1, q2, k2, q3, k3, v, wo, bo, out
                     in1=gate_exp[u][:, g, :], op0=ALU.mult, op1=ALU.mult,
                 )
             numerator[u] = flip_and_add(folded[u])
-        for b in range(B):
-            nc.vector.quantize_mx(
-                out=v_codes[:, b, :].bitcast(FP8X4), scales=v_scales[:, b, :],
-                in_=grouped[b][:].rearrange("p s j -> p (s j)"),
-            )
-        nc.vector.quantize_mx(
-            out=wo_codes[:].bitcast(FP8X4), scales=wo_scales[:], in_=grouped[B][:].rearrange("p s j -> p (s j)")
-        )
 
         attn = {}
         attn_codes = {}

@@ -123,17 +123,17 @@ def tile_channeldeattention_pa_kernel(tc, q1, k1, q2, k2, q3, k3, v, wo, bo, out
             if j == 0:
                 inverse[u] = kept.tile([P, MAPS], F32, name="inverse")
                 nc.vector.reciprocal(out=inverse[u][:], in_=sums[u][:])
-            if j == 1:
                 mean_inverse[u] = kept.tile([P, MAPS], F32, name="mean_inverse")
-                nc.vector.tensor_tensor(out=mean_inverse[u][:], in0=inverse[u][:], in1=mean_weight[:], op=ALU.mult)
+                nc.gpsimd.tensor_tensor(out=mean_inverse[u][:], in0=inverse[u][:], in1=mean_weight[:], op=ALU.mult)
                 ratio[u] = kept.tile([P, MAPS], F32, name="ratio")
                 for g in range(1, SCALES):
-                    nc.vector.tensor_scalar(
+                    nc.gpsimd.tensor_scalar(
                         out=ratio[u][:, FIRST_MAP[g] + 1 : LAST_MAP[g] + 1],
                         in0=inverse[u][:, FIRST_MAP[g] + 1 : LAST_MAP[g] + 1],
                         scalar1=sums[u][:, FIRST_MAP[g] : FIRST_MAP[g] + 1],
-                        scalar2=None,
+                        scalar2=0.0,
                         op0=ALU.mult,
+                        op1=ALU.add,
                     )
                 gate_exp[u] = kept.tile([P, SCALES, C], F32, name="gate_exp")
             if j > FIRST_MAP[i]:
@@ -184,19 +184,6 @@ def tile_channeldeattention_pa_kernel(tc, q1, k1, q2, k2, q3, k3, v, wo, bo, out
         v_scales = weights.tile([P, B, S], U8, align_bytes=64)
         wo_codes = weights.tile([P, PO], U32, align_bytes=64)
         wo_scales = weights.tile([P, PO], U8, align_bytes=64)
-        grouped = []
-        for rows in (v_raw[:, 0], v_raw[:, 1], wo_raw[:]):
-            side_by_side = weights.tile([P, S, PACK], BF16, align_bytes=64, name="side_by_side", bufs=3)
-            nc.vector.tensor_copy(out=side_by_side[:], in_=rows.rearrange("p j s -> p s j"))
-            grouped.append(side_by_side)
-        for b in range(B):
-            nc.vector.quantize_mx(
-                out=v_codes[:, b, :].bitcast(FP8X4), scales=v_scales[:, b, :],
-                in_=grouped[b][:].rearrange("p s j -> p (s j)"),
-            )
-        nc.vector.quantize_mx(
-            out=wo_codes[:].bitcast(FP8X4), scales=wo_scales[:], in_=grouped[B][:].rearrange("p s j -> p (s j)")
-        )
         bo_bank = psum.tile([P, P], BF16, tag="bank")
         nc.tensor.transpose(bo_bank[:], bo_rows[:], ident_bf[:])
         bias = consts.tile([P, PO // P], F32)
@@ -209,6 +196,11 @@ def tile_channeldeattention_pa_kernel(tc, q1, k1, q2, k2, q3, k3, v, wo, bo, out
             nc.scalar.activation(out=gate_inverse[u][:], in_=denominator[:].rearrange("p t c -> p c t"), func=ACT.Ln)
         for u in range(UNITS):
             nc.scalar.activation(out=gate_inverse[u][:], in_=gate_inverse[u][:], func=ACT.Exp, scale=-1.0)
+        grouped = []
+        for rows in (v_raw[:, 0], v_raw[:, 1], wo_raw[:]):
+            side_by_side = weights.tile([P, S, PACK], BF16, align_bytes=64, name="side_by_side", bufs=3)
+            nc.scalar.copy(out=side_by_side[:], in_=rows.rearrange("p j s -> p s j"))
+            grouped.append(side_by_side)
         numerator = {}
         for u in range(UNITS):
             for g in range(SCALES):
@@ -238,6 +230,11 @@ def tile_channeldeattention_pa_kernel(tc, q1, k1, q2, k2, q3, k3, v, wo, bo, out
             if 0 <= step - 1 < UNITS:
                 b, a = divmod(step - 1, BLOCKS)
                 cols = slice(a * P, (a + 1) * P)
+                if a == 0:
+                    nc.vector.quantize_mx(
+                        out=v_codes[:, b, :].bitcast(FP8X4), scales=v_scales[:, b, :],
+                        in_=grouped[b][:].rearrange("p s j -> p (s j)"),
+                    )
                 nc.vector.quantize_mx(
                     out=attn_codes[b][:, cols].bitcast(FP8X4), scales=attn_scales[b][:, cols],
                     in_=attn[b][:, cols, :].rearrange("p c t -> p (c t)"),
@@ -256,6 +253,11 @@ def tile_channeldeattention_pa_kernel(tc, q1, k1, q2, k2, q3, k3, v, wo, bo, out
             done = step - 1 - PROJECT_LAG
             if done >= 0 and done % BLOCKS == BLOCKS - 1:
                 b = done // BLOCKS
+                if b == 0:
+                    nc.vector.quantize_mx(
+                        out=wo_codes[:].bitcast(FP8X4), scales=wo_scales[:],
+                        in_=grouped[B][:].rearrange("p s j -> p (s j)"),
+                    )
                 h_codes = sample.tile([P, C], U32, align_bytes=64)
                 h_scales = sample.tile([P, C], U8, align_bytes=64)
                 nc.vector.quantize_mx(

@@ -123,17 +123,17 @@ def tile_channeldeattention_pa_kernel(tc, q1, k1, q2, k2, q3, k3, v, wo, bo, out
             if j == 0:
                 inverse[u] = kept.tile([P, MAPS], F32, name="inverse")
                 nc.vector.reciprocal(out=inverse[u][:], in_=sums[u][:])
+            if j == 1:
                 mean_inverse[u] = kept.tile([P, MAPS], F32, name="mean_inverse")
-                nc.gpsimd.tensor_tensor(out=mean_inverse[u][:], in0=inverse[u][:], in1=mean_weight[:], op=ALU.mult)
+                nc.vector.tensor_tensor(out=mean_inverse[u][:], in0=inverse[u][:], in1=mean_weight[:], op=ALU.mult)
                 ratio[u] = kept.tile([P, MAPS], F32, name="ratio")
                 for g in range(1, SCALES):
-                    nc.gpsimd.tensor_scalar(
+                    nc.vector.tensor_scalar(
                         out=ratio[u][:, FIRST_MAP[g] + 1 : LAST_MAP[g] + 1],
                         in0=inverse[u][:, FIRST_MAP[g] + 1 : LAST_MAP[g] + 1],
                         scalar1=sums[u][:, FIRST_MAP[g] : FIRST_MAP[g] + 1],
-                        scalar2=0.0,
+                        scalar2=None,
                         op0=ALU.mult,
-                        op1=ALU.add,
                     )
                 gate_exp[u] = kept.tile([P, SCALES, C], F32, name="gate_exp")
             if j > FIRST_MAP[i]:
@@ -196,11 +196,6 @@ def tile_channeldeattention_pa_kernel(tc, q1, k1, q2, k2, q3, k3, v, wo, bo, out
             nc.scalar.activation(out=gate_inverse[u][:], in_=denominator[:].rearrange("p t c -> p c t"), func=ACT.Ln)
         for u in range(UNITS):
             nc.scalar.activation(out=gate_inverse[u][:], in_=gate_inverse[u][:], func=ACT.Exp, scale=-1.0)
-        grouped = []
-        for rows in (v_raw[:, 0], v_raw[:, 1], wo_raw[:]):
-            side_by_side = weights.tile([P, S, PACK], BF16, align_bytes=64, name="side_by_side", bufs=3)
-            nc.scalar.copy(out=side_by_side[:], in_=rows.rearrange("p j s -> p s j"))
-            grouped.append(side_by_side)
         numerator = {}
         for u in range(UNITS):
             for g in range(SCALES):
@@ -210,6 +205,15 @@ def tile_channeldeattention_pa_kernel(tc, q1, k1, q2, k2, q3, k3, v, wo, bo, out
                     in1=gate_exp[u][:, g, :], op0=ALU.mult, op1=ALU.mult,
                 )
             numerator[u] = flip_and_add(folded[u])
+
+        grouped = []
+        for rows in (v_raw[:, 0], v_raw[:, 1], wo_raw[:]):
+            side_by_side = weights.tile([P, S, PACK], BF16, align_bytes=64, name="side_by_side", bufs=3)
+            if len(grouped) == 0:
+                nc.vector.tensor_copy(out=side_by_side[:], in_=rows.rearrange("p j s -> p s j"))
+            else:
+                nc.scalar.copy(out=side_by_side[:], in_=rows.rearrange("p j s -> p s j"))
+            grouped.append(side_by_side)
 
         attn = {}
         attn_codes = {}

@@ -29,7 +29,7 @@ TOTAL = UNITS * MAPS
 
 AHEAD = 2
 LAG = MAPS + 5
-PROJECT_LAG = 2
+PROJECT_LAG = 4
 
 FLOPS = 2 * B * MAPS * C * C * H + 2 * B * C * C * S + 2 * B * C * S * PO
 
@@ -193,9 +193,10 @@ def tile_channeldeattention_pa_kernel(tc, q1, k1, q2, k2, q3, k3, v, wo, bo, out
         for u in range(UNITS):
             denominator = flip_and_add(gate_exp[u])
             gate_inverse[u] = kept.tile([P, P, PACK], F32, name="gate_inverse")
-            nc.scalar.activation(out=gate_inverse[u][:], in_=denominator[:].rearrange("p t c -> p c t"), func=ACT.Ln)
-        for u in range(UNITS):
-            nc.scalar.activation(out=gate_inverse[u][:], in_=gate_inverse[u][:], func=ACT.Exp, scale=-1.0)
+            nc.scalar.activation(
+                out=gate_inverse[u][:], in_=denominator[:].rearrange("p t c -> p c t"), func=ACT.Abs_reciprocal_sqrt
+            )
+            nc.scalar.activation(out=gate_inverse[u][:], in_=gate_inverse[u][:], func=ACT.Square)
         numerator = {}
         for u in range(UNITS):
             for g in range(SCALES):

@@ -27,9 +27,22 @@ GROUP_OF = tuple(i for i in range(SCALES) for m in range(GROUP_SIZES[i]))
 SCORE_SCALE = 1.0 / math.sqrt(H)
 TOTAL = UNITS * MAPS
 
-AHEAD = 2
-LAG = MAPS + 5
-PROJECT_LAG = 4
+AHEAD = 4
+LAG = 13
+PROJECT_LAG = 2
+COPY_S = ((0,1),(0,3),(0,5))
+OUT0_V = ()
+OUT1_V = (4, 5, 7)
+EARLY_W = ()
+EAT = 4
+ESTEP = 4
+EPARTS = 4
+RES = 8
+REG_S = (1,)
+WOQ = 5
+QLAG = 3
+OLAG = 4
+BLOCKWISE = True
 
 FLOPS = 2 * B * MAPS * C * C * H + 2 * B * C * C * S + 2 * B * C * S * PO
 
@@ -47,7 +60,7 @@ def tile_channeldeattention_pa_kernel(tc, q1, k1, q2, k2, q3, k3, v, wo, bo, out
         stream = ctx.enter_context(tc.tile_pool(name="stream", bufs=10))
         kept = ctx.enter_context(tc.tile_pool(name="kept", bufs=UNITS))
         sample = ctx.enter_context(tc.tile_pool(name="sample", bufs=B))
-        results = ctx.enter_context(tc.tile_pool(name="results", bufs=4))
+        results = ctx.enter_context(tc.tile_pool(name="results", bufs=RES))
         psum = ctx.enter_context(tc.psum_pool(name="psum", bufs=8))
         ctx.enter_context(tc.manual_schedule())
 
@@ -75,7 +88,11 @@ def tile_channeldeattention_pa_kernel(tc, q1, k1, q2, k2, q3, k3, v, wo, bo, out
             i = GROUP_OF[j]
             n = b * GROUP_SIZES[i] + j - FIRST_MAP[i]
             q_raw = raw.tile([P, BLOCKS, H], BF16)
-            nc.sync.dma_start(out=q_raw[:], in_=queries[i][n : n + 1].rearrange("o (a p) h -> p (o a) h", p=P))
+            if b == 0:
+                view = queries[i][n : n + 1].rearrange("o (p a) h -> (o p) a h", a=BLOCKS)
+            else:
+                view = queries[i][n : n + 1].rearrange("o (a p) h -> p (o a) h", p=P)
+            nc.sync.dma_start(out=q_raw[:], in_=view)
             k_raw = raw.tile([P, PACK, H], BF16)
             nc.sync.dma_start(out=k_raw[:], in_=keys[i][n : n + 1].rearrange("o (p t) h -> (o p) t h", t=PACK))
             raw_tiles[(b, j)] = (q_raw, k_raw)
@@ -88,7 +105,10 @@ def tile_channeldeattention_pa_kernel(tc, q1, k1, q2, k2, q3, k3, v, wo, bo, out
             for t in range(PACK):
                 nc.tensor.transpose(qk_bank[:, 1, t, :], k_raw[:, t, :], ident_bf[:])
             qk_t = operands.tile([P, 2, BLOCKS, P], BF16)
-            nc.vector.tensor_copy(out=qk_t[:], in_=qk_bank[:])
+            if (b, j) in COPY_S:
+                nc.scalar.copy(out=qk_t[:], in_=qk_bank[:])
+            else:
+                nc.vector.tensor_copy(out=qk_t[:], in_=qk_bank[:])
             transposed[(b, j)] = (qk_t[:, 0], qk_t[:, 1])
 
         def score_tile(u, j):
@@ -167,7 +187,24 @@ def tile_channeldeattention_pa_kernel(tc, q1, k1, q2, k2, q3, k3, v, wo, bo, out
         nc.sync.dma_start(out=wo_raw[:], in_=wo.rearrange("(t p) n -> p t n", p=P))
         nc.sync.dma_start(out=bo_rows[0 : PO // P, :], in_=bo.rearrange("(r m) -> r m", m=P))
 
+        grouped = {}
+        weight_rows = (v_raw[:, 0], v_raw[:, 1], wo_raw[:])
+
+        def regroup(n, part, parts, on_scalar):
+            if part == 0:
+                grouped[n] = weights.tile([P, S, PACK], BF16, align_bytes=64, name="side_by_side", bufs=3)
+            columns = slice(part * (S // parts), (part + 1) * (S // parts))
+            target = grouped[n][:, columns, :].rearrange("p (c i) j -> p c j i", i=PACK)
+            source = weight_rows[n][:, :, columns].rearrange("p j (c i) -> p c j i", i=PACK)
+            if on_scalar:
+                nc.scalar.copy(out=target, in_=source)
+            else:
+                nc.vector.tensor_copy(out=target, in_=source)
+
         for step in range(-AHEAD, TOTAL + LAG):
+            done = (step - EAT) // ESTEP
+            if step >= EAT and (step - EAT) % ESTEP == 0 and done < EPARTS * len(EARLY_W):
+                regroup(EARLY_W[done // EPARTS], done % EPARTS, EPARTS, True)
             if 0 <= step < TOTAL:
                 score_tile(step // MAPS, step % MAPS)
             early = step + AHEAD
@@ -207,20 +244,50 @@ def tile_channeldeattention_pa_kernel(tc, q1, k1, q2, k2, q3, k3, v, wo, bo, out
                 )
             numerator[u] = flip_and_add(folded[u])
 
-        grouped = []
-        for rows in (v_raw[:, 0], v_raw[:, 1], wo_raw[:]):
-            side_by_side = weights.tile([P, S, PACK], BF16, align_bytes=64, name="side_by_side", bufs=3)
-            if len(grouped) == 0:
-                nc.vector.tensor_copy(out=side_by_side[:], in_=rows.rearrange("p j s -> p s j"))
-            else:
-                nc.scalar.copy(out=side_by_side[:], in_=rows.rearrange("p j s -> p s j"))
-            grouped.append(side_by_side)
+        for n in range(3):
+            if n not in EARLY_W:
+                regroup(n, 0, 1, n in REG_S)
 
         attn = {}
         attn_codes = {}
         attn_scales = {}
         hidden = {}
-        for step in range(UNITS + 1 + PROJECT_LAG):
+        out_banks = {}
+        for step in range(UNITS + 1 + max(PROJECT_LAG, OLAG)):
+            u = step - OLAG
+            if BLOCKWISE and BLOCKS <= u < UNITS:
+                b, a = divmod(u, BLOCKS)
+                result = results.tile([P, PO // P, P], F32)
+                if u in OUT1_V:
+                    nc.vector.tensor_tensor(
+                        out=result[:], in0=out_banks[u][:], in1=bias[:].unsqueeze(2).to_broadcast([P, PO // P, P]),
+                        op=ALU.add,
+                    )
+                else:
+                    for r in range(PO // P):
+                        nc.scalar.activation(
+                            out=result[:, r, :], in_=out_banks[u][:, r, :], func=ACT.Identity, bias=bias[:, r : r + 1]
+                        )
+                nc.sync.dma_start(
+                    out=out[b : b + 1, :, a * P : (a + 1) * P].rearrange("o (r p) c -> (o p) r c", p=P), in_=result[:]
+                )
+            u = step - QLAG
+            if BLOCKWISE and BLOCKS <= u < UNITS:
+                b, a = divmod(u, BLOCKS)
+                hb_codes = sample.tile([P, P], U32, align_bytes=64)
+                hb_scales = sample.tile([P, P], U8, align_bytes=64)
+                nc.vector.quantize_mx(
+                    out=hb_codes[:].bitcast(FP8X4), scales=hb_scales[:],
+                    in_=hidden[b][:, a * P : (a + 1) * P, :].rearrange("p c t -> p (c t)"),
+                )
+                out_banks[u] = psum.tile([P, PO // P, P], F32, tag="bank", name="out_bank")
+                for r in range(PO // P):
+                    nc.tensor.matmul_mx(
+                        out=out_banks[u][:, r, :],
+                        lhsT=wo_codes[:, r * P : (r + 1) * P].bitcast(FP8X4),
+                        lhsT_scale=wo_scales[:, r * P : (r + 1) * P],
+                        rhs=hb_codes[:].bitcast(FP8X4), rhs_scale=hb_scales[:], start=True, stop=True,
+                    )
             if step < UNITS:
                 b, a = divmod(step, BLOCKS)
                 if a == 0:
@@ -256,13 +323,13 @@ def tile_channeldeattention_pa_kernel(tc, q1, k1, q2, k2, q3, k3, v, wo, bo, out
                     )
                 nc.scalar.copy(out=hidden[b][:, cols, :], in_=h_bank[:].rearrange("p t c -> p c t"))
             done = step - 1 - PROJECT_LAG
-            if done >= 0 and done % BLOCKS == BLOCKS - 1:
-                b = done // BLOCKS
-                if b == 0:
+            if step == WOQ:
                     nc.vector.quantize_mx(
                         out=wo_codes[:].bitcast(FP8X4), scales=wo_scales[:],
                         in_=grouped[B][:].rearrange("p s j -> p (s j)"),
                     )
+            if done >= 0 and done % BLOCKS == BLOCKS - 1 and (not BLOCKWISE or done // BLOCKS == 0):
+                b = done // BLOCKS
                 h_codes = sample.tile([P, C], U32, align_bytes=64)
                 h_scales = sample.tile([P, C], U8, align_bytes=64)
                 nc.vector.quantize_mx(
@@ -278,13 +345,15 @@ def tile_channeldeattention_pa_kernel(tc, q1, k1, q2, k2, q3, k3, v, wo, bo, out
                         rhs_scale=h_scales[:],
                         start=True, stop=True,
                     )
-                    result = results.tile([P, C], F32)
-                    if r % 2 == 0:
-                        nc.scalar.activation(out=result[:], in_=o_bank[:], func=ACT.Identity, bias=bias[:, r : r + 1])
+                    result = results.tile([P, P, BLOCKS], F32)
+                    source = o_bank[:].rearrange("m (a p) -> m p a", a=BLOCKS)
+                    if r not in OUT0_V:
+                        nc.scalar.activation(out=result[:], in_=source, func=ACT.Identity, bias=bias[:, r : r + 1])
                     else:
                         nc.vector.tensor_scalar(
-                            out=result[:], in0=o_bank[:], scalar1=bias[:, r : r + 1], scalar2=None, op0=ALU.add
+                            out=result[:], in0=source, scalar1=bias[:, r : r + 1], scalar2=None, op0=ALU.add
                         )
                     nc.sync.dma_start(
-                        out=out[b : b + 1, r * P : (r + 1) * P, :].rearrange("o m c -> (o m) c"), in_=result[:]
+                        out=out[b : b + 1, r * P : (r + 1) * P, :].rearrange("o m c -> (o m) c"),
+                        in_=result[:].rearrange("m p a -> m (p a)"),
                     )

@@ -27,19 +27,26 @@ GROUP_OF = tuple(i for i in range(SCALES) for m in range(GROUP_SIZES[i]))
 SCORE_SCALE = 1.0 / math.sqrt(H)
 TOTAL = UNITS * MAPS
 
-AHEAD = 4
+AHEAD = 2
 LAG = 13
 PROJECT_LAG = 2
-COPY_S = ((0,1),(0,3),(0,5))
+COPY_S = ((1, 1), (1, 3), (1, 5))
 OUT0_V = ()
 OUT1_V = (4, 5, 7)
 EARLY_W = ()
 EAT = 4
 ESTEP = 4
 EPARTS = 4
-RES = 8
+RES = 4
 REG_S = (1,)
 WOQ = 5
+DENC = (26, 33, 40)
+S1 = 8
+SPB = 8
+SBB = 2
+EVQ = 50
+STR = 3
+DENL = 1
 QLAG = 3
 OLAG = 4
 BLOCKWISE = True
@@ -55,10 +62,11 @@ def tile_channeldeattention_pa_kernel(tc, q1, k1, q2, k2, q3, k3, v, wo, bo, out
     with ExitStack() as ctx:
         consts = ctx.enter_context(tc.tile_pool(name="consts", bufs=1))
         raw = ctx.enter_context(tc.tile_pool(name="raw", bufs=MAPS))
-        operands = ctx.enter_context(tc.tile_pool(name="operands", bufs=MAPS))
+        operands = ctx.enter_context(tc.tile_pool(name="operands", bufs=2 * MAPS))
         weights = ctx.enter_context(tc.tile_pool(name="weights", bufs=1))
         stream = ctx.enter_context(tc.tile_pool(name="stream", bufs=10))
         kept = ctx.enter_context(tc.tile_pool(name="kept", bufs=UNITS))
+        spares = ctx.enter_context(tc.tile_pool(name="spares", bufs=SPB))
         sample = ctx.enter_context(tc.tile_pool(name="sample", bufs=B))
         results = ctx.enter_context(tc.tile_pool(name="results", bufs=RES))
         psum = ctx.enter_context(tc.psum_pool(name="psum", bufs=8))
@@ -131,7 +139,7 @@ def tile_channeldeattention_pa_kernel(tc, q1, k1, q2, k2, q3, k3, v, wo, bo, out
             if j == FIRST_MAP[i]:
                 target = folded[u][:, i, :]
             else:
-                spare[(u, j)] = stream.tile([P, C], F32, name="spare")
+                spare[(u, j)] = spares.tile([P, C], F32, name="spare")
                 target = spare[(u, j)][:]
             nc.scalar.activation(
                 out=target, in_=scores[:], func=ACT.Exp, bias=shift[:], scale=SCORE_SCALE,
@@ -180,6 +188,8 @@ def tile_channeldeattention_pa_kernel(tc, q1, k1, q2, k2, q3, k3, v, wo, bo, out
 
         for j in range(MAPS):
             load_map(0, j)
+        v_codes = weights.tile([P, B, S], U32, align_bytes=64)
+        v_scales = weights.tile([P, B, S], U8, align_bytes=64)
         v_raw = weights.tile([P, B, PACK, S], BF16)
         for b in range(B):
             nc.sync.dma_start(out=v_raw[:, b], in_=v[b : b + 1].rearrange("o (p j) s -> (o p) j s", j=PACK))
@@ -187,12 +197,14 @@ def tile_channeldeattention_pa_kernel(tc, q1, k1, q2, k2, q3, k3, v, wo, bo, out
         nc.sync.dma_start(out=wo_raw[:], in_=wo.rearrange("(t p) n -> p t n", p=P))
         nc.sync.dma_start(out=bo_rows[0 : PO // P, :], in_=bo.rearrange("(r m) -> r m", m=P))
 
+        gate_inverse = {}
+        early_bank = {}
         grouped = {}
         weight_rows = (v_raw[:, 0], v_raw[:, 1], wo_raw[:])
 
         def regroup(n, part, parts, on_scalar):
             if part == 0:
-                grouped[n] = weights.tile([P, S, PACK], BF16, align_bytes=64, name="side_by_side", bufs=3)
+                grouped[n] = weights.tile([P, S, PACK], BF16, align_bytes=64, name="side_by_side", bufs=SBB)
             columns = slice(part * (S // parts), (part + 1) * (S // parts))
             target = grouped[n][:, columns, :].rearrange("p (c i) j -> p c j i", i=PACK)
             source = weight_rows[n][:, :, columns].rearrange("p j (c i) -> p c j i", i=PACK)
@@ -207,18 +219,30 @@ def tile_channeldeattention_pa_kernel(tc, q1, k1, q2, k2, q3, k3, v, wo, bo, out
                 regroup(EARLY_W[done // EPARTS], done % EPARTS, EPARTS, True)
             if 0 <= step < TOTAL:
                 score_tile(step // MAPS, step % MAPS)
-            early = step + AHEAD
-            if early < TOTAL and (early // MAPS) % BLOCKS == 0:
-                b, j = early // (MAPS * BLOCKS), early % MAPS
-                transpose_map(b, j)
-                if b + 1 < B:
-                    load_map(b + 1, j)
+            j = step + AHEAD
+            if j < MAPS:
+                transpose_map(0, j)
+                load_map(1, j)
+            j, rest = divmod(step - S1, STR)
+            if rest == 0 and 0 <= j < MAPS:
+                transpose_map(1, j)
+            if step == EVQ:
+                regroup(0, 0, 1, False)
+                nc.vector.quantize_mx(
+                    out=v_codes[:, 0, :].bitcast(FP8X4), scales=v_scales[:, 0, :],
+                    in_=grouped[0][:].rearrange("p s j -> p (s j)"),
+                )
+            if step in DENC:
+                u = DENC.index(step)
+                early_bank[u] = flip_and_add(gate_exp[u])
+            if step - DENL in DENC:
+                u = DENC.index(step - DENL)
+                gate_inverse[u] = kept.tile([P, P, PACK], F32, name="gate_inverse")
+                nc.scalar.copy(out=gate_inverse[u][:], in_=early_bank[u][:].rearrange("p t c -> p c t"))
             late = step - LAG
             if late >= 0:
                 fold_tile(late // MAPS, late % MAPS)
 
-        v_codes = weights.tile([P, B, S], U32, align_bytes=64)
-        v_scales = weights.tile([P, B, S], U8, align_bytes=64)
         wo_codes = weights.tile([P, PO], U32, align_bytes=64)
         wo_scales = weights.tile([P, PO], U8, align_bytes=64)
         bo_bank = psum.tile([P, P], BF16, tag="bank")
@@ -226,13 +250,14 @@ def tile_channeldeattention_pa_kernel(tc, q1, k1, q2, k2, q3, k3, v, wo, bo, out
         bias = consts.tile([P, PO // P], F32)
         nc.vector.tensor_copy(out=bias[:], in_=bo_bank[:, 0 : PO // P])
 
-        gate_inverse = {}
         for u in range(UNITS):
-            denominator = flip_and_add(gate_exp[u])
-            gate_inverse[u] = kept.tile([P, P, PACK], F32, name="gate_inverse")
-            nc.scalar.activation(
-                out=gate_inverse[u][:], in_=denominator[:].rearrange("p t c -> p c t"), func=ACT.Abs_reciprocal_sqrt
-            )
+            if u in gate_inverse:
+                source = gate_inverse[u][:]
+            else:
+                denominator = flip_and_add(gate_exp[u])
+                source = denominator[:].rearrange("p t c -> p c t")
+                gate_inverse[u] = kept.tile([P, P, PACK], F32, name="gate_inverse")
+            nc.scalar.activation(out=gate_inverse[u][:], in_=source, func=ACT.Abs_reciprocal_sqrt)
             nc.scalar.activation(out=gate_inverse[u][:], in_=gate_inverse[u][:], func=ACT.Square)
         numerator = {}
         for u in range(UNITS):
@@ -245,7 +270,7 @@ def tile_channeldeattention_pa_kernel(tc, q1, k1, q2, k2, q3, k3, v, wo, bo, out
             numerator[u] = flip_and_add(folded[u])
 
         for n in range(3):
-            if n not in EARLY_W:
+            if n > 0:
                 regroup(n, 0, 1, n in REG_S)
 
         attn = {}
@@ -302,7 +327,7 @@ def tile_channeldeattention_pa_kernel(tc, q1, k1, q2, k2, q3, k3, v, wo, bo, out
             if 0 <= step - 1 < UNITS:
                 b, a = divmod(step - 1, BLOCKS)
                 cols = slice(a * P, (a + 1) * P)
-                if a == 0:
+                if a == 0 and b > 0:
                     nc.vector.quantize_mx(
                         out=v_codes[:, b, :].bitcast(FP8X4), scales=v_scales[:, b, :],
                         in_=grouped[b][:].rearrange("p s j -> p (s j)"),

@@ -37,7 +37,7 @@ EARLY_W = ()
 EAT = 4
 ESTEP = 4
 EPARTS = 4
-RES = 4
+RES = 8
 REG_S = (1,)
 WOQ = 5
 DENC = (26, 33, 40)
@@ -45,6 +45,7 @@ S1 = 8
 SPB = 8
 SBB = 2
 EVQ = 50
+NUM_AT = ()
 STR = 3
 DENL = 1
 QLAG = 3
@@ -68,7 +69,6 @@ def tile_channeldeattention_pa_kernel(tc, q1, k1, q2, k2, q3, k3, v, wo, bo, out
         kept = ctx.enter_context(tc.tile_pool(name="kept", bufs=UNITS))
         spares = ctx.enter_context(tc.tile_pool(name="spares", bufs=SPB))
         sample = ctx.enter_context(tc.tile_pool(name="sample", bufs=B))
-        results = ctx.enter_context(tc.tile_pool(name="results", bufs=RES))
         psum = ctx.enter_context(tc.psum_pool(name="psum", bufs=8))
         ctx.enter_context(tc.manual_schedule())
 
@@ -139,7 +139,7 @@ def tile_channeldeattention_pa_kernel(tc, q1, k1, q2, k2, q3, k3, v, wo, bo, out
             if j == FIRST_MAP[i]:
                 target = folded[u][:, i, :]
             else:
-                spare[(u, j)] = spares.tile([P, C], F32, name="spare")
+                spare[(u, j)] = spares.tile([P, C], F32, tag="spare", name="spare")
                 target = spare[(u, j)][:]
             nc.scalar.activation(
                 out=target, in_=scores[:], func=ACT.Exp, bias=shift[:], scale=SCORE_SCALE,
@@ -186,6 +186,17 @@ def tile_channeldeattention_pa_kernel(tc, q1, k1, q2, k2, q3, k3, v, wo, bo, out
                     )
             return bank
 
+        numerator = {}
+
+        def multiply(u):
+            for g in range(SCALES):
+                nc.vector.scalar_tensor_tensor(
+                    out=folded[u][:, g, :], in0=folded[u][:, g, :],
+                    scalar=mean_inverse[u][:, FIRST_MAP[g] : FIRST_MAP[g] + 1],
+                    in1=gate_exp[u][:, g, :], op0=ALU.mult, op1=ALU.mult,
+                )
+            numerator[u] = flip_and_add(folded[u])
+
         for j in range(MAPS):
             load_map(0, j)
         v_codes = weights.tile([P, B, S], U32, align_bytes=64)
@@ -226,6 +237,8 @@ def tile_channeldeattention_pa_kernel(tc, q1, k1, q2, k2, q3, k3, v, wo, bo, out
             j, rest = divmod(step - S1, STR)
             if rest == 0 and 0 <= j < MAPS:
                 transpose_map(1, j)
+            if step in NUM_AT:
+                multiply(NUM_AT.index(step))
             if step == EVQ:
                 regroup(0, 0, 1, False)
                 nc.vector.quantize_mx(
@@ -259,15 +272,9 @@ def tile_channeldeattention_pa_kernel(tc, q1, k1, q2, k2, q3, k3, v, wo, bo, out
                 gate_inverse[u] = kept.tile([P, P, PACK], F32, name="gate_inverse")
             nc.scalar.activation(out=gate_inverse[u][:], in_=source, func=ACT.Abs_reciprocal_sqrt)
             nc.scalar.activation(out=gate_inverse[u][:], in_=gate_inverse[u][:], func=ACT.Square)
-        numerator = {}
         for u in range(UNITS):
-            for g in range(SCALES):
-                nc.vector.scalar_tensor_tensor(
-                    out=folded[u][:, g, :], in0=folded[u][:, g, :],
-                    scalar=mean_inverse[u][:, FIRST_MAP[g] : FIRST_MAP[g] + 1],
-                    in1=gate_exp[u][:, g, :], op0=ALU.mult, op1=ALU.mult,
-                )
-            numerator[u] = flip_and_add(folded[u])
+            if u not in numerator:
+                multiply(u)
 
         for n in range(3):
             if n > 0:
@@ -282,7 +289,7 @@ def tile_channeldeattention_pa_kernel(tc, q1, k1, q2, k2, q3, k3, v, wo, bo, out
             u = step - OLAG
             if BLOCKWISE and BLOCKS <= u < UNITS:
                 b, a = divmod(u, BLOCKS)
-                result = results.tile([P, PO // P, P], F32)
+                result = spares.tile([P, PO // P, P], F32, tag="spare")
                 if u in OUT1_V:
                     nc.vector.tensor_tensor(
                         out=result[:], in0=out_banks[u][:], in1=bias[:].unsqueeze(2).to_broadcast([P, PO // P, P]),
@@ -370,7 +377,7 @@ def tile_channeldeattention_pa_kernel(tc, q1, k1, q2, k2, q3, k3, v, wo, bo, out
                         rhs_scale=h_scales[:],
                         start=True, stop=True,
                     )
-                    result = results.tile([P, P, BLOCKS], F32)
+                    result = spares.tile([P, P, BLOCKS], F32, tag="spare")
                     source = o_bank[:].rearrange("m (a p) -> m p a", a=BLOCKS)
                     if r not in OUT0_V:
                         nc.scalar.activation(out=result[:], in_=source, func=ACT.Identity, bias=bias[:, r : r + 1])

@@ -27,7 +27,7 @@ GROUP_OF = tuple(i for i in range(SCALES) for m in range(GROUP_SIZES[i]))
 SCORE_SCALE = 1.0 / math.sqrt(H)
 TOTAL = UNITS * MAPS
 
-AHEAD = 2
+AHEAD = 3
 LAG = 13
 PROJECT_LAG = 2
 COPY_S = ((1, 1), (1, 3), (1, 5))
@@ -46,6 +46,8 @@ SPB = 8
 SBB = 2
 EVQ = 50
 NUM_AT = ()
+FIRST_BLOCKS = (0,)
+REST = 3
 STR = 3
 DENL = 1
 QLAG = 3
@@ -105,19 +107,26 @@ def tile_channeldeattention_pa_kernel(tc, q1, k1, q2, k2, q3, k3, v, wo, bo, out
             nc.sync.dma_start(out=k_raw[:], in_=keys[i][n : n + 1].rearrange("o (p t) h -> (o p) t h", t=PACK))
             raw_tiles[(b, j)] = (q_raw, k_raw)
 
-        def transpose_map(b, j):
+        def transpose_map(b, j, blocks, keys_too):
             q_raw, k_raw = raw_tiles[(b, j)]
-            qk_bank = psum.tile([P, 2, BLOCKS, P], BF16, tag="bank")
-            for a in range(BLOCKS):
-                nc.tensor.transpose(qk_bank[:, 0, a, :], q_raw[:, a, :], ident_bf[:])
-            for t in range(PACK):
-                nc.tensor.transpose(qk_bank[:, 1, t, :], k_raw[:, t, :], ident_bf[:])
-            qk_t = operands.tile([P, 2, BLOCKS, P], BF16)
+            n = len(blocks) + (PACK if keys_too else 0)
+            qk_bank = psum.tile([P, 2 * BLOCKS, P], BF16, tag="bank")
+            place = 0
+            if keys_too:
+                for t in range(PACK):
+                    nc.tensor.transpose(qk_bank[:, t, :], k_raw[:, t, :], ident_bf[:])
+                place = PACK
+            for a in blocks:
+                nc.tensor.transpose(qk_bank[:, place, :], q_raw[:, a, :], ident_bf[:])
+                place += 1
+            if keys_too:
+                transposed[(b, j)] = operands.tile([P, 2 * BLOCKS, P], BF16, name="transposed")
+            first = 0 if keys_too else PACK + blocks[0]
+            target = transposed[(b, j)][:, first : first + n, :]
             if (b, j) in COPY_S:
-                nc.scalar.copy(out=qk_t[:], in_=qk_bank[:])
+                nc.scalar.copy(out=target, in_=qk_bank[:, 0:n, :])
             else:
-                nc.vector.tensor_copy(out=qk_t[:], in_=qk_bank[:])
-            transposed[(b, j)] = (qk_t[:, 0], qk_t[:, 1])
+                nc.vector.tensor_copy(out=target, in_=qk_bank[:, 0:n, :])
 
         def score_tile(u, j):
             b, a = divmod(u, BLOCKS)
@@ -125,7 +134,8 @@ def tile_channeldeattention_pa_kernel(tc, q1, k1, q2, k2, q3, k3, v, wo, bo, out
             if j == 0:
                 sums[u] = kept.tile([P, MAPS], F32, name="sums")
                 folded[u] = kept.tile([P, SCALES, C], F32, name="folded")
-            q_t, k_t = transposed[(b, j)]
+            q_t = transposed[(b, j)][:, PACK:, :]
+            k_t = transposed[(b, j)][:, 0:PACK, :]
             scores = psum.tile([P, C], F32, tag="bank")
             nc.tensor.matmul(
                 out=scores[:], lhsT=q_t[:, a, :], rhs=k_t.rearrange("h t c -> h (t c)"), start=True, stop=True
@@ -232,11 +242,14 @@ def tile_channeldeattention_pa_kernel(tc, q1, k1, q2, k2, q3, k3, v, wo, bo, out
                 score_tile(step // MAPS, step % MAPS)
             j = step + AHEAD
             if j < MAPS:
-                transpose_map(0, j)
-                load_map(1, j)
+                transpose_map(0, j, FIRST_BLOCKS, True)
+            if len(FIRST_BLOCKS) < BLOCKS and 0 <= step - REST < MAPS:
+                transpose_map(0, step - REST, tuple(range(len(FIRST_BLOCKS), BLOCKS)), False)
+            if 0 <= step - REST < MAPS:
+                load_map(1, step - REST)
             j, rest = divmod(step - S1, STR)
             if rest == 0 and 0 <= j < MAPS:
-                transpose_map(1, j)
+                transpose_map(1, j, (0, 1, 2, 3), True)
             if step in NUM_AT:
                 multiply(NUM_AT.index(step))
             if step == EVQ:

from contextlib import ExitStack
import math

import concourse.mybir as mybir
from concourse.masks import make_identity

F32 = mybir.dt.float32
BF16 = mybir.dt.bfloat16
U32 = mybir.dt.uint32
U8 = mybir.dt.uint8
FP8X4 = mybir.dt.float8_e4m3fn_x4
ACT = mybir.ActivationFunctionType
ALU = mybir.AluOpType
AXIS = mybir.AxisListType

P = 128
PACK = 4
B, C, H, S, PO = 2, 512, 128, 512, 512
BLOCKS = C // P
UNITS = B * BLOCKS
GROUP_SIZES = (1, 2, 4)
SCALES = len(GROUP_SIZES)
MAPS = sum(GROUP_SIZES)
FIRST_MAP = tuple(sum(GROUP_SIZES[:i]) for i in range(SCALES))
LAST_MAP = tuple(FIRST_MAP[i] + GROUP_SIZES[i] - 1 for i in range(SCALES))
GROUP_OF = tuple(i for i in range(SCALES) for m in range(GROUP_SIZES[i]))
SCORE_SCALE = 1.0 / math.sqrt(H)
TOTAL = UNITS * MAPS

AHEAD = 3
LAG = 13
PROJECT_LAG = 2
COPY_S = ((1, 1), (1, 3), (1, 5))
OUT0_V = ()
OUT1_V = (4, 5, 7)
EARLY_W = ()
EAT = 4
ESTEP = 4
EPARTS = 4
RES = 8
REG_S = (1,)
WOQ = 5
DENC = (26, 33, 40)
S1 = 8
SPB = 8
SBB = 2
EVQ = 50
NUM_AT = ()
FIRST_BLOCKS = (0,)
REST = 3
STR = 3
DENL = 1
QLAG = 3
OLAG = 4
BLOCKWISE = True

FLOPS = 2 * B * MAPS * C * C * H + 2 * B * C * C * S + 2 * B * C * S * PO


def tile_channeldeattention_pa_kernel(tc, q1, k1, q2, k2, q3, k3, v, wo, bo, out):
    nc = tc.nc
    queries = (q1, q2, q3)
    keys = (k1, k2, k3)

    with ExitStack() as ctx:
        consts = ctx.enter_context(tc.tile_pool(name="consts", bufs=1))
        raw = ctx.enter_context(tc.tile_pool(name="raw", bufs=MAPS))
        operands = ctx.enter_context(tc.tile_pool(name="operands", bufs=2 * MAPS))
        weights = ctx.enter_context(tc.tile_pool(name="weights", bufs=1))
        stream = ctx.enter_context(tc.tile_pool(name="stream", bufs=10))
        kept = ctx.enter_context(tc.tile_pool(name="kept", bufs=UNITS))
        spares = ctx.enter_context(tc.tile_pool(name="spares", bufs=SPB))
        sample = ctx.enter_context(tc.tile_pool(name="sample", bufs=B))
        psum = ctx.enter_context(tc.psum_pool(name="psum", bufs=8))
        ctx.enter_context(tc.manual_schedule())

        ident_bf = consts.tile([P, P], BF16)
        make_identity(nc, ident_bf[:])
        ident_f = consts.tile([P, P], F32)
        make_identity(nc, ident_f[:])
        mean_weight = consts.tile([P, MAPS], F32)
        for i in range(SCALES):
            nc.vector.memset(mean_weight[:, FIRST_MAP[i] : LAST_MAP[i] + 1], 1.0 / GROUP_SIZES[i])
        bo_rows = consts.tile([P, P], BF16)
        nc.vector.memset(bo_rows[:], 0.0)

        raw_tiles = {}
        transposed = {}
        sums = {}
        mean_inverse = {}
        ratio = {}
        inverse = {}
        folded = {}
        gate_exp = {}
        spare = {}

        def load_map(b, j):
            i = GROUP_OF[j]
            n = b * GROUP_SIZES[i] + j - FIRST_MAP[i]
            q_raw = raw.tile([P, BLOCKS, H], BF16)
            if b == 0:
                view = queries[i][n : n + 1].rearrange("o (p a) h -> (o p) a h", a=BLOCKS)
            else:
                view = queries[i][n : n + 1].rearrange("o (a p) h -> p (o a) h", p=P)
            nc.sync.dma_start(out=q_raw[:], in_=view)
            k_raw = raw.tile([P, PACK, H], BF16)
            nc.sync.dma_start(out=k_raw[:], in_=keys[i][n : n + 1].rearrange("o (p t) h -> (o p) t h", t=PACK))
            raw_tiles[(b, j)] = (q_raw, k_raw)

        def transpose_map(b, j, blocks, keys_too):
            q_raw, k_raw = raw_tiles[(b, j)]
            n = len(blocks) + (PACK if keys_too else 0)
            qk_bank = psum.tile([P, 2 * BLOCKS, P], BF16, tag="bank")
            place = 0
            if keys_too:
                for t in range(PACK):
                    nc.tensor.transpose(qk_bank[:, t, :], k_raw[:, t, :], ident_bf[:])
                place = PACK
            for a in blocks:
                nc.tensor.transpose(qk_bank[:, place, :], q_raw[:, a, :], ident_bf[:])
                place += 1
            if keys_too:
                transposed[(b, j)] = operands.tile([P, 2 * BLOCKS, P], BF16, name="transposed")
            first = 0 if keys_too else PACK + blocks[0]
            target = transposed[(b, j)][:, first : first + n, :]
            if (b, j) in COPY_S:
                nc.scalar.copy(out=target, in_=qk_bank[:, 0:n, :])
            else:
                nc.vector.tensor_copy(out=target, in_=qk_bank[:, 0:n, :])

        def score_tile(u, j):
            b, a = divmod(u, BLOCKS)
            i = GROUP_OF[j]
            if j == 0:
                sums[u] = kept.tile([P, MAPS], F32, name="sums")
                folded[u] = kept.tile([P, SCALES, C], F32, name="folded")
            q_t = transposed[(b, j)][:, PACK:, :]
            k_t = transposed[(b, j)][:, 0:PACK, :]
            scores = psum.tile([P, C], F32, tag="bank")
            nc.tensor.matmul(
                out=scores[:], lhsT=q_t[:, a, :], rhs=k_t.rearrange("h t c -> h (t c)"), start=True, stop=True
            )
            row_max = stream.tile([P, 1], F32)
            nc.vector.tensor_reduce(out=row_max[:], in_=scores[:], axis=AXIS.X, op=ALU.max)
            shift = stream.tile([P, 1], F32)
            nc.gpsimd.tensor_scalar(
                out=shift[:], in0=row_max[:], scalar1=-SCORE_SCALE, scalar2=0.0, op0=ALU.mult, op1=ALU.add
            )
            if j == FIRST_MAP[i]:
                target = folded[u][:, i, :]
            else:
                spare[(u, j)] = spares.tile([P, C], F32, tag="spare", name="spare")
                target = spare[(u, j)][:]
            nc.scalar.activation(
                out=target, in_=scores[:], func=ACT.Exp, bias=shift[:], scale=SCORE_SCALE,
                accum_out=sums[u][:, j : j + 1],
            )

        def fold_tile(u, j):
            i = GROUP_OF[j]
            if j == 0:
                inverse[u] = kept.tile([P, MAPS], F32, name="inverse")
                nc.vector.reciprocal(out=inverse[u][:], in_=sums[u][:])
            if j == 1:
                mean_inverse[u] = kept.tile([P, MAPS], F32, name="mean_inverse")
                nc.vector.tensor_tensor(out=mean_inverse[u][:], in0=inverse[u][:], in1=mean_weight[:], op=ALU.mult)
                ratio[u] = kept.tile([P, MAPS], F32, name="ratio")
                for g in range(1, SCALES):
                    nc.vector.tensor_scalar(
                        out=ratio[u][:, FIRST_MAP[g] + 1 : LAST_MAP[g] + 1],
                        in0=inverse[u][:, FIRST_MAP[g] + 1 : LAST_MAP[g] + 1],
                        scalar1=sums[u][:, FIRST_MAP[g] : FIRST_MAP[g] + 1],
                        scalar2=None,
                        op0=ALU.mult,
                    )
                gate_exp[u] = kept.tile([P, SCALES, C], F32, name="gate_exp")
            if j > FIRST_MAP[i]:
                nc.vector.scalar_tensor_tensor(
                    out=folded[u][:, i, :], in0=spare[(u, j)][:], scalar=ratio[u][:, j : j + 1],
                    in1=folded[u][:, i, :], op0=ALU.mult, op1=ALU.add,
                )
            for g in range(SCALES):
                if j == max(LAST_MAP[g], 1):
                    nc.scalar.activation(
                        out=gate_exp[u][:, g, :], in_=folded[u][:, g, :], func=ACT.Exp,
                        scale=mean_inverse[u][:, FIRST_MAP[g] : FIRST_MAP[g] + 1],
                    )

        def flip_and_add(three_maps):
            bank = psum.tile([P, PACK, P], F32, tag="bank", name="flipped")
            for t in range(PACK):
                for g in range(SCALES):
                    nc.tensor.matmul(
                        out=bank[:, t, :], lhsT=three_maps[:, g, t * P : (t + 1) * P], rhs=ident_f[:],
                        is_transpose=True, start=(g == 0), stop=(g == SCALES - 1),
                    )
            return bank

        numerator = {}

        def multiply(u):
            for g in range(SCALES):
                nc.vector.scalar_tensor_tensor(
                    out=folded[u][:, g, :], in0=folded[u][:, g, :],
                    scalar=mean_inverse[u][:, FIRST_MAP[g] : FIRST_MAP[g] + 1],
                    in1=gate_exp[u][:, g, :], op0=ALU.mult, op1=ALU.mult,
                )
            numerator[u] = flip_and_add(folded[u])

        for j in range(MAPS):
            load_map(0, j)
        v_codes = weights.tile([P, B, S], U32, align_bytes=64)
        v_scales = weights.tile([P, B, S], U8, align_bytes=64)
        v_raw = weights.tile([P, B, PACK, S], BF16)
        for b in range(B):
            nc.sync.dma_start(out=v_raw[:, b], in_=v[b : b + 1].rearrange("o (p j) s -> (o p) j s", j=PACK))
        wo_raw = weights.tile([P, PACK, PO], BF16)
        nc.sync.dma_start(out=wo_raw[:], in_=wo.rearrange("(t p) n -> p t n", p=P))
        nc.sync.dma_start(out=bo_rows[0 : PO // P, :], in_=bo.rearrange("(r m) -> r m", m=P))

        gate_inverse = {}
        early_bank = {}
        grouped = {}
        weight_rows = (v_raw[:, 0], v_raw[:, 1], wo_raw[:])

        def regroup(n, part, parts, on_scalar):
            if part == 0:
                grouped[n] = weights.tile([P, S, PACK], BF16, align_bytes=64, name="side_by_side", bufs=SBB)
            columns = slice(part * (S // parts), (part + 1) * (S // parts))
            target = grouped[n][:, columns, :].rearrange("p (c i) j -> p c j i", i=PACK)
            source = weight_rows[n][:, :, columns].rearrange("p j (c i) -> p c j i", i=PACK)
            if on_scalar:
                nc.scalar.copy(out=target, in_=source)
            else:
                nc.vector.tensor_copy(out=target, in_=source)

        for step in range(-AHEAD, TOTAL + LAG):
            done = (step - EAT) // ESTEP
            if step >= EAT and (step - EAT) % ESTEP == 0 and done < EPARTS * len(EARLY_W):
                regroup(EARLY_W[done // EPARTS], done % EPARTS, EPARTS, True)
            if 0 <= step < TOTAL:
                score_tile(step // MAPS, step % MAPS)
            j = step + AHEAD
            if j < MAPS:
                transpose_map(0, j, FIRST_BLOCKS, True)
            if len(FIRST_BLOCKS) < BLOCKS and 0 <= step - REST < MAPS:
                transpose_map(0, step - REST, tuple(range(len(FIRST_BLOCKS), BLOCKS)), False)
            if 0 <= step - REST < MAPS:
                load_map(1, step - REST)
            j, rest = divmod(step - S1, STR)
            if rest == 0 and 0 <= j < MAPS:
                transpose_map(1, j, (0, 1, 2, 3), True)
            if step in NUM_AT:
                multiply(NUM_AT.index(step))
            if step == EVQ:
                regroup(0, 0, 1, False)
                nc.vector.quantize_mx(
                    out=v_codes[:, 0, :].bitcast(FP8X4), scales=v_scales[:, 0, :],
                    in_=grouped[0][:].rearrange("p s j -> p (s j)"),
                )
            if step in DENC:
                u = DENC.index(step)
                early_bank[u] = flip_and_add(gate_exp[u])
            if step - DENL in DENC:
                u = DENC.index(step - DENL)
                gate_inverse[u] = kept.tile([P, P, PACK], F32, name="gate_inverse")
                nc.scalar.copy(out=gate_inverse[u][:], in_=early_bank[u][:].rearrange("p t c -> p c t"))
            late = step - LAG
            if late >= 0:
                fold_tile(late // MAPS, late % MAPS)

        wo_codes = weights.tile([P, PO], U32, align_bytes=64)
        wo_scales = weights.tile([P, PO], U8, align_bytes=64)
        bo_bank = psum.tile([P, P], BF16, tag="bank")
        nc.tensor.transpose(bo_bank[:], bo_rows[:], ident_bf[:])
        bias = consts.tile([P, PO // P], F32)
        nc.vector.tensor_copy(out=bias[:], in_=bo_bank[:, 0 : PO // P])

        for u in range(UNITS):
            if u in gate_inverse:
                source = gate_inverse[u][:]
            else:
                denominator = flip_and_add(gate_exp[u])
                source = denominator[:].rearrange("p t c -> p c t")
                gate_inverse[u] = kept.tile([P, P, PACK], F32, name="gate_inverse")
            nc.scalar.activation(out=gate_inverse[u][:], in_=source, func=ACT.Abs_reciprocal_sqrt)
            nc.scalar.activation(out=gate_inverse[u][:], in_=gate_inverse[u][:], func=ACT.Square)
        for u in range(UNITS):
            if u not in numerator:
                multiply(u)

        for n in range(3):
            if n > 0:
                regroup(n, 0, 1, n in REG_S)

        attn = {}
        attn_codes = {}
        attn_scales = {}
        hidden = {}
        out_banks = {}
        for step in range(UNITS + 1 + max(PROJECT_LAG, OLAG)):
            u = step - OLAG
            if BLOCKWISE and BLOCKS <= u < UNITS:
                b, a = divmod(u, BLOCKS)
                result = spares.tile([P, PO // P, P], F32, tag="spare")
                if u in OUT1_V:
                    nc.vector.tensor_tensor(
                        out=result[:], in0=out_banks[u][:], in1=bias[:].unsqueeze(2).to_broadcast([P, PO // P, P]),
                        op=ALU.add,
                    )
                else:
                    for r in range(PO // P):
                        nc.scalar.activation(
                            out=result[:, r, :], in_=out_banks[u][:, r, :], func=ACT.Identity, bias=bias[:, r : r + 1]
                        )
                nc.sync.dma_start(
                    out=out[b : b + 1, :, a * P : (a + 1) * P].rearrange("o (r p) c -> (o p) r c", p=P), in_=result[:]
                )
            u = step - QLAG
            if BLOCKWISE and BLOCKS <= u < UNITS:
                b, a = divmod(u, BLOCKS)
                hb_codes = sample.tile([P, P], U32, align_bytes=64)
                hb_scales = sample.tile([P, P], U8, align_bytes=64)
                nc.vector.quantize_mx(
                    out=hb_codes[:].bitcast(FP8X4), scales=hb_scales[:],
                    in_=hidden[b][:, a * P : (a + 1) * P, :].rearrange("p c t -> p (c t)"),
                )
                out_banks[u] = psum.tile([P, PO // P, P], F32, tag="bank", name="out_bank")
                for r in range(PO // P):
                    nc.tensor.matmul_mx(
                        out=out_banks[u][:, r, :],
                        lhsT=wo_codes[:, r * P : (r + 1) * P].bitcast(FP8X4),
                        lhsT_scale=wo_scales[:, r * P : (r + 1) * P],
                        rhs=hb_codes[:].bitcast(FP8X4), rhs_scale=hb_scales[:], start=True, stop=True,
                    )
            if step < UNITS:
                b, a = divmod(step, BLOCKS)
                if a == 0:
                    attn[b] = sample.tile([P, C, PACK], BF16, align_bytes=64, name="attn")
                    attn_codes[b] = sample.tile([P, C], U32, align_bytes=64, name="attn_codes")
                    attn_scales[b] = sample.tile([P, C], U8, align_bytes=64, name="attn_scales")
                    hidden[b] = sample.tile([P, C, PACK], BF16, align_bytes=64, name="hidden")
                nc.vector.tensor_tensor(
                    out=attn[b][:, a * P : (a + 1) * P, :], in0=numerator[step][:].rearrange("p t c -> p c t"),
                    in1=gate_inverse[step][:], op=ALU.mult,
                )
            if 0 <= step - 1 < UNITS:
                b, a = divmod(step - 1, BLOCKS)
                cols = slice(a * P, (a + 1) * P)
                if a == 0 and b > 0:
                    nc.vector.quantize_mx(
                        out=v_codes[:, b, :].bitcast(FP8X4), scales=v_scales[:, b, :],
                        in_=grouped[b][:].rearrange("p s j -> p (s j)"),
                    )
                nc.vector.quantize_mx(
                    out=attn_codes[b][:, cols].bitcast(FP8X4), scales=attn_scales[b][:, cols],
                    in_=attn[b][:, cols, :].rearrange("p c t -> p (c t)"),
                )
                h_bank = psum.tile([P, PACK, P], F32, tag="bank")
                for t in range(PACK):
                    nc.tensor.matmul_mx(
                        out=h_bank[:, t, :],
                        lhsT=v_codes[:, b, t * P : (t + 1) * P].bitcast(FP8X4),
                        lhsT_scale=v_scales[:, b, t * P : (t + 1) * P],
                        rhs=attn_codes[b][:, cols].bitcast(FP8X4),
                        rhs_scale=attn_scales[b][:, cols],
                        start=True, stop=True,
                    )
                nc.scalar.copy(out=hidden[b][:, cols, :], in_=h_bank[:].rearrange("p t c -> p c t"))
            done = step - 1 - PROJECT_LAG
            if step == WOQ:
                    nc.vector.quantize_mx(
                        out=wo_codes[:].bitcast(FP8X4), scales=wo_scales[:],
                        in_=grouped[B][:].rearrange("p s j -> p (s j)"),
                    )
            if done >= 0 and done % BLOCKS == BLOCKS - 1 and (not BLOCKWISE or done // BLOCKS == 0):
                b = done // BLOCKS
                h_codes = sample.tile([P, C], U32, align_bytes=64)
                h_scales = sample.tile([P, C], U8, align_bytes=64)
                nc.vector.quantize_mx(
                    out=h_codes[:].bitcast(FP8X4), scales=h_scales[:], in_=hidden[b][:].rearrange("p c t -> p (c t)")
                )
                for r in range(PO // P):
                    o_bank = psum.tile([P, C], F32, tag="bank")
                    nc.tensor.matmul_mx(
                        out=o_bank[:],
                        lhsT=wo_codes[:, r * P : (r + 1) * P].bitcast(FP8X4),
                        lhsT_scale=wo_scales[:, r * P : (r + 1) * P],
                        rhs=h_codes[:].bitcast(FP8X4),
                        rhs_scale=h_scales[:],
                        start=True, stop=True,
                    )
                    result = spares.tile([P, P, BLOCKS], F32, tag="spare")
                    source = o_bank[:].rearrange("m (a p) -> m p a", a=BLOCKS)
                    if r not in OUT0_V:
                        nc.scalar.activation(out=result[:], in_=source, func=ACT.Identity, bias=bias[:, r : r + 1])
                    else:
                        nc.vector.tensor_scalar(
                            out=result[:], in0=source, scalar1=bias[:, r : r + 1], scalar2=None, op0=ALU.add
                        )
                    nc.sync.dma_start(
                        out=out[b : b + 1, r * P : (r + 1) * P, :].rearrange("o m c -> (o m) c"),
                        in_=result[:].rearrange("m p a -> m (p a)"),
                    )
